import numpy as np
import ml_dtypes


def mxq(x, axis, fmt="e4m3"):
    dtype, down = {"e4m3": (ml_dtypes.float8_e4m3fn, 7), "e5m2": (ml_dtypes.float8_e5m2, 14)}[fmt]
    v = np.moveaxis(np.asarray(x, np.float32).astype(ml_dtypes.bfloat16).astype(np.float64), axis, -1)
    blocks = v.reshape(v.shape[:-1] + (-1, 32))
    amax = np.abs(blocks).max(-1, keepdims=True)
    byte = np.maximum(np.where(amax > 0, np.frexp(amax)[1] - 1 + 127, 0) - down, 1)
    scale = np.exp2(byte - 127.0)
    codes = (blocks / scale).astype(np.float32).astype(dtype).astype(np.float64)
    return np.moveaxis((codes * scale).reshape(v.shape), -1, axis)


WIDE = False


def mx_kscale(k):
    if not WIDE:
        return np.ones(k)
    levels = np.array([10, -10, 5, -5, 0])
    a = np.random.permutation(np.resize(levels, k // 512 * 4)).reshape(k // 512, 4)
    idx = np.arange(k)
    return np.exp2(a[idx // 512, idx % 128 // 32])


BF16 = ml_dtypes.bfloat16


def bf(x):
    return np.asarray(x, np.float32).astype(BF16)


def f64(x):
    return np.asarray(x).astype(np.float64)


B, S, D, H, QL, KL, ND, VD, RD = 4, 256, 2048, 16, 512, 512, 128, 128, 128
BASE = 10000.0


def rope(v):
    d = v.shape[-1]
    inv_freq = BASE ** (-np.arange(0, d, 2) / d)
    ang = np.arange(v.shape[1])[:, None] * inv_freq[None, :]
    cos = np.cos(ang)[None, :, None, :]
    sin = np.sin(ang)[None, :, None, :]
    v1 = v[..., 0::2]
    v2 = v[..., 1::2]
    o1 = v1 * cos - v2 * sin
    o2 = v1 * sin + v2 * cos
    return np.stack([o1, o2], axis=-1).reshape(v.shape)


def setup_inputs():
    s, t = mx_kscale(D), mx_kscale(KL)
    tc = np.concatenate([t, np.ones(RD)])
    return {"x": bf(np.random.standard_normal((B, S, D)) * s),
            "Wkva": bf(np.random.standard_normal((D, KL + RD)) / np.sqrt(D) / s[:, None] * tc),
            "Wkvb": bf(np.random.standard_normal((KL, H * (ND + VD))) / np.sqrt(KL) / t[:, None])}


def reference(x, Wkva, Wkvb):
    ckv = mxq(f64(x), 2, "e4m3") @ mxq(f64(Wkva), 0, "e4m3")
    compressed_kv, k_pe = ckv[..., :KL], ckv[..., KL:]
    k_pe = np.broadcast_to(k_pe[:, :, None, :], (B, S, H, RD))
    kv = (mxq(compressed_kv, 2, "e4m3") @ mxq(f64(Wkvb), 0, "e4m3")).reshape(B, S, H, ND + VD)
    k_nope, v = kv[..., :ND], kv[..., ND:]
    kf = np.concatenate([k_nope, rope(k_pe)], axis=-1)
    return kf, v

@@ -1,0 +1,269 @@
+import math
+from contextlib import ExitStack
+
+import concourse.mybir as mybir
+from concourse.masks import make_identity
+
+BF16 = mybir.dt.bfloat16
+F32 = mybir.dt.float32
+U32 = mybir.dt.uint32
+U8 = mybir.dt.uint8
+FP8X4 = mybir.dt.float8_e4m3fn_x4
+ALU = mybir.AluOpType
+
+P = 128
+PACK = 4
+K_PASS = P * PACK
+BANK = 512
+
+TOKENS = 4 * 256
+POSITIONS = 256
+D_MODEL = 2048
+HEADS = 16
+LATENT = 512
+ROPE = 128
+NOPE = 128
+VDIM = 128
+ROPE_BASE = 10000.0
+
+TOKEN_TILES = TOKENS // P
+X_PASSES = D_MODEL // K_PASS
+PAIRS = ROPE // 2
+HEAD_GROUP = BANK // NOPE
+HEAD_GROUPS = HEADS // HEAD_GROUP
+UNIT = BANK * PACK
+ROUND_MAGIC = 1.5 * 2.0**23
+
+FLOPS = 2 * TOKENS * D_MODEL * (LATENT + ROPE) + 2 * TOKENS * LATENT * HEADS * (NOPE + VDIM)
+
+
+def span(index, width):
+    return slice(index * width, (index + 1) * width)
+
+
+def tile_multilatentattention_pb_kernel(tc, x, Wkva, Wkvb, out_0, out_1):
+    nc = tc.nc
+    x_rows = x.flatten_outer_dims()
+    kf_rows = out_0.rearrange("b s h d -> (b s) (h d)")
+    v_rows = out_1.rearrange("b s h d -> (b s) (h d)")
+
+    with ExitStack() as ctx:
+        const = ctx.enter_context(tc.tile_pool(name="const", bufs=1))
+        raw = ctx.enter_context(tc.tile_pool(name="raw", bufs=1))
+        stage = ctx.enter_context(tc.tile_pool(name="stage", bufs=3))
+        x_pool = ctx.enter_context(tc.tile_pool(name="x_pool", bufs=2))
+        c_pool = ctx.enter_context(tc.tile_pool(name="c_pool", bufs=3))
+        rope_pool = ctx.enter_context(tc.tile_pool(name="rope_pool", bufs=2))
+        out_pool = ctx.enter_context(tc.tile_pool(name="out_pool", bufs=2))
+        psum_x = ctx.enter_context(tc.psum_pool(name="psum_x", bufs=2))
+        psum_c = ctx.enter_context(tc.psum_pool(name="psum_c", bufs=1))
+        psum_kv = ctx.enter_context(tc.psum_pool(name="psum_kv", bufs=4))
+
+        x_raw = [raw.tile([P, D_MODEL], BF16, name="x_raw%d" % i) for i in range(TOKEN_TILES)]
+        wa_raw = raw.tile([P, X_PASSES, PACK, LATENT + ROPE], BF16)
+        wb_raw = raw.tile([P, HEAD_GROUPS, PACK, HEAD_GROUP * (NOPE + VDIM)], BF16)
+        nc.sync.dma_start(out=x_raw[0][:], in_=x_rows[span(0, P), :])
+        for g in range(X_PASSES):
+            nc.sync.dma_start(
+                out=wa_raw[:, g, :, :], in_=Wkva[span(g, K_PASS), :].rearrange("(p j) c -> p j c", j=PACK)
+            )
+        wb_by_partition = Wkvb.rearrange("(t p) n -> p t n", p=P)
+        for q in range(HEAD_GROUPS):
+            nc.sync.dma_start(
+                out=wb_raw[:, q, :, :], in_=wb_by_partition[:, :, span(q, HEAD_GROUP * (NOPE + VDIM))]
+            )
+        for i in range(1, TOKEN_TILES):
+            nc.sync.dma_start(out=x_raw[i][:], in_=x_rows[span(i, P), :])
+
+        ident = const.tile([P, P], F32)
+        make_identity(nc, ident[:])
+
+        freq = const.tile([P, PAIRS], F32)
+        nc.vector.memset(freq[:, 0:1], 1.0)
+        for doubling in range(6):
+            w = 2**doubling
+            nc.vector.tensor_scalar(
+                out=freq[:, w : 2 * w],
+                in0=freq[:, 0:w],
+                scalar1=ROPE_BASE ** (-2.0 * w / ROPE),
+                scalar2=None,
+                op0=ALU.mult,
+            )
+        position = const.tile([P, 2], F32)
+        nc.gpsimd.iota(
+            position[:], pattern=[[P, 2]], base=0, channel_multiplier=1, allow_small_or_imprecise_dtypes=True
+        )
+        turns = const.tile([P, 2 * 2 * PAIRS], F32)
+        turns_view = turns[:].rearrange("p (f h j) -> p f h j", f=2, h=2)
+        for half in range(2):
+            nc.vector.tensor_scalar(
+                out=turns_view[:, 0, half, :],
+                in0=freq[:],
+                scalar1=position[:, half : half + 1],
+                scalar2=1.0 / (2.0 * math.pi),
+                op0=ALU.mult,
+                op1=ALU.mult,
+            )
+        nc.vector.tensor_scalar(
+            out=turns[:, 2 * PAIRS :], in0=turns[:, : 2 * PAIRS], scalar1=0.25, scalar2=None, op0=ALU.add
+        )
+        whole_turns = const.tile([P, 2 * 2 * PAIRS], F32)
+        nc.vector.tensor_scalar(
+            out=whole_turns[:],
+            in0=turns[:],
+            scalar1=ROUND_MAGIC,
+            scalar2=ROUND_MAGIC,
+            op0=ALU.add,
+            op1=ALU.subtract,
+        )
+        part_turns = const.tile([P, 2 * 2 * PAIRS], F32)
+        nc.vector.tensor_tensor(out=part_turns[:], in0=turns[:], in1=whole_turns[:], op=ALU.subtract)
+        trig = const.tile([P, 2 * 2 * PAIRS], F32)
+        nc.scalar.activation(
+            out=trig[:], in_=part_turns[:], func=mybir.ActivationFunctionType.Sin, scale=2.0 * math.pi
+        )
+        trig_view = trig[:].rearrange("p (f h j) -> p f h j", f=2, h=2)
+
+        wa_codes = const.tile([P, X_PASSES * LATENT], U32, align_bytes=64)
+        wa_scales = const.tile([P, X_PASSES * LATENT], U8, align_bytes=64)
+        wr_codes = const.tile([P, X_PASSES * ROPE], U32, align_bytes=64)
+        wr_scales = const.tile([P, X_PASSES * ROPE], U8, align_bytes=64)
+        wb_codes = const.tile([P, 2 * HEADS * NOPE], U32, align_bytes=64)
+        wb_scales = const.tile([P, 2 * HEADS * NOPE], U8, align_bytes=64)
+
+        def quantise_unit(vector_half, scalar_half, codes, scales):
+            grouped = stage.tile([P, UNIT], BF16, align_bytes=64)
+            targets = grouped[:].rearrange("p (s n c j) -> p s n c j", s=2, n=2, j=PACK)
+            nc.vector.tensor_copy(out=targets[:, 0], in_=vector_half)
+            nc.scalar.copy(out=targets[:, 1], in_=scalar_half)
+            nc.vector.quantize_mx(out=codes.bitcast(FP8X4), scales=scales, in_=grouped[:])
+
+        def quantise_wkva():
+            for g in range(X_PASSES):
+                latent = wa_raw[:, g, :, :LATENT].rearrange("p j (n c) -> p n c j", c=P)
+                quantise_unit(
+                    latent[:, 0:2], latent[:, 2:4], wa_codes[:, span(g, LATENT)], wa_scales[:, span(g, LATENT)]
+                )
+            rope = wa_raw[:, :, :, LATENT:].rearrange("p g j c -> p g c j")
+            quantise_unit(rope[:, 0:2], rope[:, 2:4], wr_codes[:], wr_scales[:])
+
+        def quantise_wkvb():
+            for kind in range(2):
+                for q in range(HEAD_GROUPS):
+                    heads = wb_raw[:, q, :, :].rearrange("p t (h k c) -> p k h c t", k=2, c=NOPE)[:, kind]
+                    quantise_unit(
+                        heads[:, 0:2],
+                        heads[:, 2:4],
+                        wb_codes[:, span(kind * HEAD_GROUPS + q, BANK)],
+                        wb_scales[:, span(kind * HEAD_GROUPS + q, BANK)],
+                    )
+
+        x_quantised = {}
+        c_quantised = {}
+        kf_tiles = {}
+
+        def prepare(i):
+            words = x_raw[i][:].bitcast(F32).rearrange("r (g p u) -> r g u p", g=X_PASSES, u=2)
+            x_grouped = x_pool.tile([P, D_MODEL], BF16, align_bytes=64)
+            grouped_words = x_grouped[:].bitcast(F32).rearrange("p (g r u) -> p g r u", g=X_PASSES, u=2)
+            for bank in range(2):
+                x_t = psum_x.tile([P, 2, 2, P], F32)
+                for g in range(2):
+                    for u in range(2):
+                        nc.tensor.transpose(out=x_t[:, g, u, :], in_=words[:, 2 * bank + g, u, :], identity=ident[:])
+                nc.vector.tensor_copy(
+                    out=grouped_words[:, span(bank, 2), :, :], in_=x_t[:].rearrange("p g u r -> p g r u")
+                )
+            x_codes = x_pool.tile([P, X_PASSES * P], U32, align_bytes=64)
+            x_scales = x_pool.tile([P, X_PASSES * P], U8, align_bytes=64)
+            nc.vector.quantize_mx(out=x_codes[:].bitcast(FP8X4), scales=x_scales[:], in_=x_grouped[:])
+            x_quantised[i] = (x_codes, x_scales)
+
+        def project(i):
+            x_codes, x_scales = x_quantised[i]
+            c_t = psum_c.tile([P, PACK, P], F32)
+            for t in range(PACK):
+                for g in range(X_PASSES):
+                    nc.tensor.matmul_mx(
+                        out=c_t[:, t, :],
+                        lhsT=wa_codes[:, span(g * PACK + t, P)].bitcast(FP8X4),
+                        lhsT_scale=wa_scales[:, span(g * PACK + t, P)],
+                        rhs=x_codes[:, span(g, P)].bitcast(FP8X4),
+                        rhs_scale=x_scales[:, span(g, P)],
+                        start=(g == 0),
+                        stop=(g == X_PASSES - 1),
+                    )
+            k_pe = psum_c.tile([P, ROPE], F32)
+            for g in range(X_PASSES):
+                nc.tensor.matmul_mx(
+                    out=k_pe[:],
+                    lhsT=x_codes[:, span(g, P)].bitcast(FP8X4),
+                    lhsT_scale=x_scales[:, span(g, P)],
+                    rhs=wr_codes[:, span(g, ROPE)].bitcast(FP8X4),
+                    rhs_scale=wr_scales[:, span(g, ROPE)],
+                    start=(g == 0),
+                    stop=(g == X_PASSES - 1),
+                )
+            c_grouped = c_pool.tile([P, P, PACK], BF16, align_bytes=64)
+            nc.vector.tensor_copy(out=c_grouped[:], in_=c_t[:].rearrange("p t r -> p r t"))
+            c_codes = c_pool.tile([P, P], U32, align_bytes=64)
+            c_scales = c_pool.tile([P, P], U8, align_bytes=64)
+            nc.vector.quantize_mx(
+                out=c_codes[:].bitcast(FP8X4), scales=c_scales[:], in_=c_grouped[:].rearrange("p r t -> p (r t)")
+            )
+            c_quantised[i] = (c_codes, c_scales)
+
+            half = i % 2
+            sin = trig_view[:, 0, half, :].unsqueeze(2).to_broadcast([P, PAIRS, 2])
+            cos = trig_view[:, 1, half, :].unsqueeze(2).to_broadcast([P, PAIRS, 2])
+            pairs = k_pe[:].rearrange("p (j e) -> p j e", e=2)
+            by_cos = rope_pool.tile([P, PAIRS, 2], F32)
+            by_sin = rope_pool.tile([P, PAIRS, 2], F32)
+            rotated = rope_pool.tile([P, PAIRS, 2], F32)
+            nc.vector.tensor_tensor(out=by_cos[:], in0=pairs, in1=cos, op=ALU.mult)
+            nc.vector.tensor_tensor(out=by_sin[:], in0=pairs, in1=sin, op=ALU.mult)
+            nc.vector.tensor_tensor(out=rotated[:, :, 0], in0=by_cos[:, :, 0], in1=by_sin[:, :, 1], op=ALU.subtract)
+            nc.vector.tensor_tensor(out=rotated[:, :, 1], in0=by_sin[:, :, 0], in1=by_cos[:, :, 1], op=ALU.add)
+            kf_tile = out_pool.tile([P, HEADS, NOPE + ROPE], F32, bufs=3)
+            nc.vector.tensor_copy(
+                out=kf_tile[:, :, NOPE:],
+                in_=rotated[:].rearrange("p j e -> p (j e)").unsqueeze(1).to_broadcast([P, HEADS, ROPE]),
+            )
+            kf_tiles[i] = kf_tile
+
+        def expand(i):
+            c_codes, c_scales = c_quantised[i]
+            kf_tile = kf_tiles[i]
+            v_tile = out_pool.tile([P, HEADS, VDIM], F32)
+            for kind in range(2):
+                for q in range(HEAD_GROUPS):
+                    kv = psum_kv.tile([P, HEAD_GROUP, NOPE], F32)
+                    nc.tensor.matmul_mx(
+                        out=kv[:].rearrange("p h c -> p (h c)"),
+                        lhsT=c_codes[:].bitcast(FP8X4),
+                        lhsT_scale=c_scales[:],
+                        rhs=wb_codes[:, span(kind * HEAD_GROUPS + q, BANK)].bitcast(FP8X4),
+                        rhs_scale=wb_scales[:, span(kind * HEAD_GROUPS + q, BANK)],
+                        start=True,
+                        stop=True,
+                    )
+                    if kind == 0:
+                        nc.scalar.copy(out=kf_tile[:, span(q, HEAD_GROUP), :NOPE], in_=kv[:])
+                    else:
+                        nc.scalar.copy(out=v_tile[:, span(q, HEAD_GROUP), :], in_=kv[:])
+                if kind == 0:
+                    nc.sync.dma_start(out=kf_rows[span(i, P), :], in_=kf_tile[:].rearrange("p h d -> p (h d)"))
+                else:
+                    nc.sync.dma_start(out=v_rows[span(i, P), :], in_=v_tile[:].rearrange("p h d -> p (h d)"))
+
+        prepare(0)
+        quantise_wkva()
+        project(0)
+        prepare(1)
+        quantise_wkvb()
+        for i in range(TOKEN_TILES):
+            if i + 2 < TOKEN_TILES:
+                prepare(i + 2)
+            if i + 1 < TOKEN_TILES:
+                project(i + 1)
+            expand(i)

@@ -32,6 +32,9 @@ PAIRS = ROPE // 2
 HEAD_GROUP = BANK // NOPE
 HEAD_GROUPS = HEADS // HEAD_GROUP
 UNIT = BANK * PACK
+VECTOR_COLUMNS = 64
+K_NOPE, V_PART = 0, 1
+LEAD = 3
 ROUND_MAGIC = 1.5 * 2.0**23
 
 FLOPS = 2 * TOKENS * D_MODEL * (LATENT + ROPE) + 2 * TOKENS * LATENT * HEADS * (NOPE + VDIM)
@@ -52,9 +55,9 @@ def tile_multilatentattention_pb_kernel(tc, x, Wkva, Wkvb, out_0, out_1):
         raw = ctx.enter_context(tc.tile_pool(name="raw", bufs=1))
         stage = ctx.enter_context(tc.tile_pool(name="stage", bufs=3))
         x_pool = ctx.enter_context(tc.tile_pool(name="x_pool", bufs=2))
-        c_pool = ctx.enter_context(tc.tile_pool(name="c_pool", bufs=3))
+        c_pool = ctx.enter_context(tc.tile_pool(name="c_pool", bufs=2))
         rope_pool = ctx.enter_context(tc.tile_pool(name="rope_pool", bufs=2))
-        out_pool = ctx.enter_context(tc.tile_pool(name="out_pool", bufs=2))
+        out_pool = ctx.enter_context(tc.tile_pool(name="out_pool", bufs=3))
         psum_x = ctx.enter_context(tc.psum_pool(name="psum_x", bufs=2))
         psum_c = ctx.enter_context(tc.psum_pool(name="psum_c", bufs=1))
         psum_kv = ctx.enter_context(tc.psum_pool(name="psum_kv", bufs=4))
@@ -131,32 +134,29 @@ def tile_multilatentattention_pb_kernel(tc, x, Wkva, Wkvb, out_0, out_1):
         wb_codes = const.tile([P, 2 * HEADS * NOPE], U32, align_bytes=64)
         wb_scales = const.tile([P, 2 * HEADS * NOPE], U8, align_bytes=64)
 
-        def quantise_unit(vector_half, scalar_half, codes, scales):
+        def quantise_unit(columns, codes, scales):
             grouped = stage.tile([P, UNIT], BF16, align_bytes=64)
-            targets = grouped[:].rearrange("p (s n c j) -> p s n c j", s=2, n=2, j=PACK)
-            nc.vector.tensor_copy(out=targets[:, 0], in_=vector_half)
-            nc.scalar.copy(out=targets[:, 1], in_=scalar_half)
+            target = grouped[:].rearrange("p (n c j) -> p n c j", n=4, j=PACK)
+            nc.vector.tensor_copy(out=target[:, :, :VECTOR_COLUMNS, :], in_=columns[:, :, :VECTOR_COLUMNS, :])
+            nc.scalar.copy(out=target[:, :, VECTOR_COLUMNS:, :], in_=columns[:, :, VECTOR_COLUMNS:, :])
             nc.vector.quantize_mx(out=codes.bitcast(FP8X4), scales=scales, in_=grouped[:])
 
         def quantise_wkva():
             for g in range(X_PASSES):
-                latent = wa_raw[:, g, :, :LATENT].rearrange("p j (n c) -> p n c j", c=P)
                 quantise_unit(
-                    latent[:, 0:2], latent[:, 2:4], wa_codes[:, span(g, LATENT)], wa_scales[:, span(g, LATENT)]
+                    wa_raw[:, g, :, :LATENT].rearrange("p j (n c) -> p n c j", c=P),
+                    wa_codes[:, span(g, LATENT)],
+                    wa_scales[:, span(g, LATENT)],
                 )
-            rope = wa_raw[:, :, :, LATENT:].rearrange("p g j c -> p g c j")
-            quantise_unit(rope[:, 0:2], rope[:, 2:4], wr_codes[:], wr_scales[:])
+            quantise_unit(wa_raw[:, :, :, LATENT:].rearrange("p g j c -> p g c j"), wr_codes[:], wr_scales[:])
 
-        def quantise_wkvb():
-            for kind in range(2):
-                for q in range(HEAD_GROUPS):
-                    heads = wb_raw[:, q, :, :].rearrange("p t (h k c) -> p k h c t", k=2, c=NOPE)[:, kind]
-                    quantise_unit(
-                        heads[:, 0:2],
-                        heads[:, 2:4],
-                        wb_codes[:, span(kind * HEAD_GROUPS + q, BANK)],
-                        wb_scales[:, span(kind * HEAD_GROUPS + q, BANK)],
-                    )
+        def quantise_wkvb(kind):
+            for q in range(HEAD_GROUPS):
+                quantise_unit(
+                    wb_raw[:, q, :, :].rearrange("p t (h k c) -> p k h c t", k=2, c=NOPE)[:, kind],
+                    wb_codes[:, span(kind * HEAD_GROUPS + q, BANK)],
+                    wb_scales[:, span(kind * HEAD_GROUPS + q, BANK)],
+                )
 
         x_quantised = {}
         c_quantised = {}
@@ -171,7 +171,7 @@ def tile_multilatentattention_pb_kernel(tc, x, Wkva, Wkvb, out_0, out_1):
                 for g in range(2):
                     for u in range(2):
                         nc.tensor.transpose(out=x_t[:, g, u, :], in_=words[:, 2 * bank + g, u, :], identity=ident[:])
-                nc.vector.tensor_copy(
+                nc.scalar.copy(
                     out=grouped_words[:, span(bank, 2), :, :], in_=x_t[:].rearrange("p g u r -> p g r u")
                 )
             x_codes = x_pool.tile([P, X_PASSES * P], U32, align_bytes=64)
@@ -206,8 +206,8 @@ def tile_multilatentattention_pb_kernel(tc, x, Wkva, Wkvb, out_0, out_1):
                 )
             c_grouped = c_pool.tile([P, P, PACK], BF16, align_bytes=64)
             nc.vector.tensor_copy(out=c_grouped[:], in_=c_t[:].rearrange("p t r -> p r t"))
-            c_codes = c_pool.tile([P, P], U32, align_bytes=64)
-            c_scales = c_pool.tile([P, P], U8, align_bytes=64)
+            c_codes = const.tile([P, P], U32, align_bytes=64, name="c_codes%d" % i)
+            c_scales = const.tile([P, P], U8, align_bytes=64, name="c_scales%d" % i)
             nc.vector.quantize_mx(
                 out=c_codes[:].bitcast(FP8X4), scales=c_scales[:], in_=c_grouped[:].rearrange("p r t -> p (r t)")
             )
@@ -224,46 +224,54 @@ def tile_multilatentattention_pb_kernel(tc, x, Wkva, Wkvb, out_0, out_1):
             nc.vector.tensor_tensor(out=by_sin[:], in0=pairs, in1=sin, op=ALU.mult)
             nc.vector.tensor_tensor(out=rotated[:, :, 0], in0=by_cos[:, :, 0], in1=by_sin[:, :, 1], op=ALU.subtract)
             nc.vector.tensor_tensor(out=rotated[:, :, 1], in0=by_sin[:, :, 0], in1=by_cos[:, :, 1], op=ALU.add)
-            kf_tile = out_pool.tile([P, HEADS, NOPE + ROPE], F32, bufs=3)
+            kf_tile = out_pool.tile([P, HEADS, NOPE + ROPE], F32)
             nc.vector.tensor_copy(
                 out=kf_tile[:, :, NOPE:],
                 in_=rotated[:].rearrange("p j e -> p (j e)").unsqueeze(1).to_broadcast([P, HEADS, ROPE]),
             )
             kf_tiles[i] = kf_tile
 
-        def expand(i):
+        def expand(i, kind):
             c_codes, c_scales = c_quantised[i]
-            kf_tile = kf_tiles[i]
-            v_tile = out_pool.tile([P, HEADS, VDIM], F32)
-            for kind in range(2):
-                for q in range(HEAD_GROUPS):
-                    kv = psum_kv.tile([P, HEAD_GROUP, NOPE], F32)
-                    nc.tensor.matmul_mx(
-                        out=kv[:].rearrange("p h c -> p (h c)"),
-                        lhsT=c_codes[:].bitcast(FP8X4),
-                        lhsT_scale=c_scales[:],
-                        rhs=wb_codes[:, span(kind * HEAD_GROUPS + q, BANK)].bitcast(FP8X4),
-                        rhs_scale=wb_scales[:, span(kind * HEAD_GROUPS + q, BANK)],
-                        start=True,
-                        stop=True,
-                    )
-                    if kind == 0:
-                        nc.scalar.copy(out=kf_tile[:, span(q, HEAD_GROUP), :NOPE], in_=kv[:])
-                    else:
-                        nc.scalar.copy(out=v_tile[:, span(q, HEAD_GROUP), :], in_=kv[:])
-                if kind == 0:
-                    nc.sync.dma_start(out=kf_rows[span(i, P), :], in_=kf_tile[:].rearrange("p h d -> p (h d)"))
+            if kind == K_NOPE:
+                out_tile = kf_tiles[i]
+                out_rows = kf_rows
+            else:
+                out_tile = out_pool.tile([P, HEADS, VDIM], F32, name="v_tile")
+                out_rows = v_rows
+            for q in range(HEAD_GROUPS):
+                kv = psum_kv.tile([P, HEAD_GROUP, NOPE], F32)
+                nc.tensor.matmul_mx(
+                    out=kv[:].rearrange("p h c -> p (h c)"),
+                    lhsT=c_codes[:].bitcast(FP8X4),
+                    lhsT_scale=c_scales[:],
+                    rhs=wb_codes[:, span(kind * HEAD_GROUPS + q, BANK)].bitcast(FP8X4),
+                    rhs_scale=wb_scales[:, span(kind * HEAD_GROUPS + q, BANK)],
+                    start=True,
+                    stop=True,
+                )
+                if kind == K_NOPE or q % 2 == 0:
+                    nc.scalar.copy(out=out_tile[:, span(q, HEAD_GROUP), :NOPE], in_=kv[:])
                 else:
-                    nc.sync.dma_start(out=v_rows[span(i, P), :], in_=v_tile[:].rearrange("p h d -> p (h d)"))
+                    nc.vector.tensor_copy(out=out_tile[:, span(q, HEAD_GROUP), :NOPE], in_=kv[:])
+            nc.sync.dma_start(out=out_rows[span(i, P), :], in_=out_tile[:].rearrange("p h d -> p (h d)"))
+
+        def next_tile(i):
+            if i + 1 < TOKEN_TILES:
+                prepare(i + 1)
+                project(i + 1)
 
         prepare(0)
         quantise_wkva()
         project(0)
-        prepare(1)
-        quantise_wkvb()
-        for i in range(TOKEN_TILES):
-            if i + 2 < TOKEN_TILES:
-                prepare(i + 2)
-            if i + 1 < TOKEN_TILES:
-                project(i + 1)
-            expand(i)
+        quantise_wkvb(K_NOPE)
+        for i in range(LEAD):
+            next_tile(i)
+            expand(i, K_NOPE)
+        quantise_wkvb(V_PART)
+        for i in range(LEAD):
+            expand(i, V_PART)
+        for i in range(LEAD, TOKEN_TILES):
+            next_tile(i)
+            expand(i, K_NOPE)
+            expand(i, V_PART)

@@ -32,9 +32,8 @@ PAIRS = ROPE // 2
 HEAD_GROUP = BANK // NOPE
 HEAD_GROUPS = HEADS // HEAD_GROUP
 UNIT = BANK * PACK
-VECTOR_COLUMNS = 64
-K_NOPE, V_PART = 0, 1
-LEAD = 3
+RUN = 4
+WB_PIECES = 2
 ROUND_MAGIC = 1.5 * 2.0**23
 
 FLOPS = 2 * TOKENS * D_MODEL * (LATENT + ROPE) + 2 * TOKENS * LATENT * HEADS * (NOPE + VDIM)
@@ -55,25 +54,26 @@ def tile_multilatentattention_pb_kernel(tc, x, Wkva, Wkvb, out_0, out_1):
         raw = ctx.enter_context(tc.tile_pool(name="raw", bufs=1))
         stage = ctx.enter_context(tc.tile_pool(name="stage", bufs=3))
         x_pool = ctx.enter_context(tc.tile_pool(name="x_pool", bufs=2))
-        c_pool = ctx.enter_context(tc.tile_pool(name="c_pool", bufs=2))
+        c_pool = ctx.enter_context(tc.tile_pool(name="c_pool", bufs=3))
         rope_pool = ctx.enter_context(tc.tile_pool(name="rope_pool", bufs=2))
-        out_pool = ctx.enter_context(tc.tile_pool(name="out_pool", bufs=3))
+        out_pool = ctx.enter_context(tc.tile_pool(name="out_pool", bufs=2))
         psum_x = ctx.enter_context(tc.psum_pool(name="psum_x", bufs=2))
         psum_c = ctx.enter_context(tc.psum_pool(name="psum_c", bufs=1))
         psum_kv = ctx.enter_context(tc.psum_pool(name="psum_kv", bufs=4))
 
         x_raw = [raw.tile([P, D_MODEL], BF16, name="x_raw%d" % i) for i in range(TOKEN_TILES)]
         wa_raw = raw.tile([P, X_PASSES, PACK, LATENT + ROPE], BF16)
-        wb_raw = raw.tile([P, HEAD_GROUPS, PACK, HEAD_GROUP * (NOPE + VDIM)], BF16)
+        wb_raw = raw.tile([P, WB_PIECES, PACK, HEADS // WB_PIECES * (NOPE + VDIM)], BF16)
         nc.sync.dma_start(out=x_raw[0][:], in_=x_rows[span(0, P), :])
         for g in range(X_PASSES):
             nc.sync.dma_start(
                 out=wa_raw[:, g, :, :], in_=Wkva[span(g, K_PASS), :].rearrange("(p j) c -> p j c", j=PACK)
             )
         wb_by_partition = Wkvb.rearrange("(t p) n -> p t n", p=P)
-        for q in range(HEAD_GROUPS):
+        for piece in range(WB_PIECES):
             nc.sync.dma_start(
-                out=wb_raw[:, q, :, :], in_=wb_by_partition[:, :, span(q, HEAD_GROUP * (NOPE + VDIM))]
+                out=wb_raw[:, piece, :, :],
+                in_=wb_by_partition[:, :, span(piece, HEADS // WB_PIECES * (NOPE + VDIM))],
             )
         for i in range(1, TOKEN_TILES):
             nc.sync.dma_start(out=x_raw[i][:], in_=x_rows[span(i, P), :])
@@ -136,9 +136,11 @@ def tile_multilatentattention_pb_kernel(tc, x, Wkva, Wkvb, out_0, out_1):
 
         def quantise_unit(columns, codes, scales):
             grouped = stage.tile([P, UNIT], BF16, align_bytes=64)
-            target = grouped[:].rearrange("p (n c j) -> p n c j", n=4, j=PACK)
-            nc.vector.tensor_copy(out=target[:, :, :VECTOR_COLUMNS, :], in_=columns[:, :, :VECTOR_COLUMNS, :])
-            nc.scalar.copy(out=target[:, :, VECTOR_COLUMNS:, :], in_=columns[:, :, VECTOR_COLUMNS:, :])
+            target = grouped[:].rearrange("p (n c i j) -> p n c j i", n=4, i=RUN, j=PACK)
+            source = columns.rearrange("p n (c i) j -> p n c j i", i=RUN)
+            nc.vector.tensor_copy(out=target[:, 0:2], in_=source[:, 0:2])
+            for n in range(2, 4):
+                nc.scalar.copy(out=target[:, n], in_=source[:, n])
             nc.vector.quantize_mx(out=codes.bitcast(FP8X4), scales=scales, in_=grouped[:])
 
         def quantise_wkva():
@@ -150,13 +152,16 @@ def tile_multilatentattention_pb_kernel(tc, x, Wkva, Wkvb, out_0, out_1):
                 )
             quantise_unit(wa_raw[:, :, :, LATENT:].rearrange("p g j c -> p g c j"), wr_codes[:], wr_scales[:])
 
-        def quantise_wkvb(kind):
-            for q in range(HEAD_GROUPS):
-                quantise_unit(
-                    wb_raw[:, q, :, :].rearrange("p t (h k c) -> p k h c t", k=2, c=NOPE)[:, kind],
-                    wb_codes[:, span(kind * HEAD_GROUPS + q, BANK)],
-                    wb_scales[:, span(kind * HEAD_GROUPS + q, BANK)],
-                )
+        def quantise_wkvb():
+            groups = HEAD_GROUPS // WB_PIECES
+            for kind in range(2):
+                for q in range(HEAD_GROUPS):
+                    heads = wb_raw[:, q // groups, :, :].rearrange("p t (h k c) -> p k h c t", k=2, c=NOPE)
+                    quantise_unit(
+                        heads[:, kind, span(q % groups, HEAD_GROUP)],
+                        wb_codes[:, span(kind * HEAD_GROUPS + q, BANK)],
+                        wb_scales[:, span(kind * HEAD_GROUPS + q, BANK)],
+                    )
 
         x_quantised = {}
         c_quantised = {}
@@ -171,7 +176,7 @@ def tile_multilatentattention_pb_kernel(tc, x, Wkva, Wkvb, out_0, out_1):
                 for g in range(2):
                     for u in range(2):
                         nc.tensor.transpose(out=x_t[:, g, u, :], in_=words[:, 2 * bank + g, u, :], identity=ident[:])
-                nc.scalar.copy(
+                nc.vector.tensor_copy(
                     out=grouped_words[:, span(bank, 2), :, :], in_=x_t[:].rearrange("p g u r -> p g r u")
                 )
             x_codes = x_pool.tile([P, X_PASSES * P], U32, align_bytes=64)
@@ -206,8 +211,8 @@ def tile_multilatentattention_pb_kernel(tc, x, Wkva, Wkvb, out_0, out_1):
                 )
             c_grouped = c_pool.tile([P, P, PACK], BF16, align_bytes=64)
             nc.vector.tensor_copy(out=c_grouped[:], in_=c_t[:].rearrange("p t r -> p r t"))
-            c_codes = const.tile([P, P], U32, align_bytes=64, name="c_codes%d" % i)
-            c_scales = const.tile([P, P], U8, align_bytes=64, name="c_scales%d" % i)
+            c_codes = c_pool.tile([P, P], U32, align_bytes=64)
+            c_scales = c_pool.tile([P, P], U8, align_bytes=64)
             nc.vector.quantize_mx(
                 out=c_codes[:].bitcast(FP8X4), scales=c_scales[:], in_=c_grouped[:].rearrange("p r t -> p (r t)")
             )
@@ -224,54 +229,46 @@ def tile_multilatentattention_pb_kernel(tc, x, Wkva, Wkvb, out_0, out_1):
             nc.vector.tensor_tensor(out=by_sin[:], in0=pairs, in1=sin, op=ALU.mult)
             nc.vector.tensor_tensor(out=rotated[:, :, 0], in0=by_cos[:, :, 0], in1=by_sin[:, :, 1], op=ALU.subtract)
             nc.vector.tensor_tensor(out=rotated[:, :, 1], in0=by_sin[:, :, 0], in1=by_cos[:, :, 1], op=ALU.add)
-            kf_tile = out_pool.tile([P, HEADS, NOPE + ROPE], F32)
+            kf_tile = out_pool.tile([P, HEADS, NOPE + ROPE], F32, bufs=3)
             nc.vector.tensor_copy(
                 out=kf_tile[:, :, NOPE:],
                 in_=rotated[:].rearrange("p j e -> p (j e)").unsqueeze(1).to_broadcast([P, HEADS, ROPE]),
             )
             kf_tiles[i] = kf_tile
 
-        def expand(i, kind):
+        def expand(i):
             c_codes, c_scales = c_quantised[i]
-            if kind == K_NOPE:
-                out_tile = kf_tiles[i]
-                out_rows = kf_rows
-            else:
-                out_tile = out_pool.tile([P, HEADS, VDIM], F32, name="v_tile")
-                out_rows = v_rows
-            for q in range(HEAD_GROUPS):
-                kv = psum_kv.tile([P, HEAD_GROUP, NOPE], F32)
-                nc.tensor.matmul_mx(
-                    out=kv[:].rearrange("p h c -> p (h c)"),
-                    lhsT=c_codes[:].bitcast(FP8X4),
-                    lhsT_scale=c_scales[:],
-                    rhs=wb_codes[:, span(kind * HEAD_GROUPS + q, BANK)].bitcast(FP8X4),
-                    rhs_scale=wb_scales[:, span(kind * HEAD_GROUPS + q, BANK)],
-                    start=True,
-                    stop=True,
-                )
-                if kind == K_NOPE or q % 2 == 0:
-                    nc.scalar.copy(out=out_tile[:, span(q, HEAD_GROUP), :NOPE], in_=kv[:])
+            kf_tile = kf_tiles[i]
+            v_tile = out_pool.tile([P, HEADS, VDIM], F32)
+            for kind in range(2):
+                for q in range(HEAD_GROUPS):
+                    kv = psum_kv.tile([P, HEAD_GROUP, NOPE], F32)
+                    nc.tensor.matmul_mx(
+                        out=kv[:].rearrange("p h c -> p (h c)"),
+                        lhsT=c_codes[:].bitcast(FP8X4),
+                        lhsT_scale=c_scales[:],
+                        rhs=wb_codes[:, span(kind * HEAD_GROUPS + q, BANK)].bitcast(FP8X4),
+                        rhs_scale=wb_scales[:, span(kind * HEAD_GROUPS + q, BANK)],
+                        start=True,
+                        stop=True,
+                    )
+                    if kind == 0:
+                        nc.scalar.copy(out=kf_tile[:, span(q, HEAD_GROUP), :NOPE], in_=kv[:])
+                    else:
+                        nc.scalar.copy(out=v_tile[:, span(q, HEAD_GROUP), :], in_=kv[:])
+                if kind == 0:
+                    nc.sync.dma_start(out=kf_rows[span(i, P), :], in_=kf_tile[:].rearrange("p h d -> p (h d)"))
                 else:
-                    nc.vector.tensor_copy(out=out_tile[:, span(q, HEAD_GROUP), :NOPE], in_=kv[:])
-            nc.sync.dma_start(out=out_rows[span(i, P), :], in_=out_tile[:].rearrange("p h d -> p (h d)"))
-
-        def next_tile(i):
-            if i + 1 < TOKEN_TILES:
-                prepare(i + 1)
-                project(i + 1)
+                    nc.sync.dma_start(out=v_rows[span(i, P), :], in_=v_tile[:].rearrange("p h d -> p (h d)"))
 
         prepare(0)
         quantise_wkva()
         project(0)
-        quantise_wkvb(K_NOPE)
-        for i in range(LEAD):
-            next_tile(i)
-            expand(i, K_NOPE)
-        quantise_wkvb(V_PART)
-        for i in range(LEAD):
-            expand(i, V_PART)
-        for i in range(LEAD, TOKEN_TILES):
-            next_tile(i)
-            expand(i, K_NOPE)
-            expand(i, V_PART)
+        prepare(1)
+        quantise_wkvb()
+        for i in range(TOKEN_TILES):
+            if i + 2 < TOKEN_TILES:
+                prepare(i + 2)
+            if i + 1 < TOKEN_TILES:
+                project(i + 1)
+            expand(i)

import math
from contextlib import ExitStack

import concourse.mybir as mybir
from concourse.masks import make_identity

BF16 = mybir.dt.bfloat16
F32 = mybir.dt.float32
U32 = mybir.dt.uint32
U8 = mybir.dt.uint8
FP8X4 = mybir.dt.float8_e4m3fn_x4
ALU = mybir.AluOpType

P = 128
PACK = 4
K_PASS = P * PACK
BANK = 512

TOKENS = 4 * 256
POSITIONS = 256
D_MODEL = 2048
HEADS = 16
LATENT = 512
ROPE = 128
NOPE = 128
VDIM = 128
ROPE_BASE = 10000.0

TOKEN_TILES = TOKENS // P
X_PASSES = D_MODEL // K_PASS
PAIRS = ROPE // 2
HEAD_GROUP = BANK // NOPE
HEAD_GROUPS = HEADS // HEAD_GROUP
UNIT = BANK * PACK
RUN = 4
WB_PIECES = 2
ROUND_MAGIC = 1.5 * 2.0**23

FLOPS = 2 * TOKENS * D_MODEL * (LATENT + ROPE) + 2 * TOKENS * LATENT * HEADS * (NOPE + VDIM)


def span(index, width):
    return slice(index * width, (index + 1) * width)


def tile_multilatentattention_pb_kernel(tc, x, Wkva, Wkvb, out_0, out_1):
    nc = tc.nc
    x_rows = x.flatten_outer_dims()
    kf_rows = out_0.rearrange("b s h d -> (b s) (h d)")
    v_rows = out_1.rearrange("b s h d -> (b s) (h d)")

    with ExitStack() as ctx:
        const = ctx.enter_context(tc.tile_pool(name="const", bufs=1))
        raw = ctx.enter_context(tc.tile_pool(name="raw", bufs=1))
        stage = ctx.enter_context(tc.tile_pool(name="stage", bufs=3))
        x_pool = ctx.enter_context(tc.tile_pool(name="x_pool", bufs=2))
        c_pool = ctx.enter_context(tc.tile_pool(name="c_pool", bufs=3))
        rope_pool = ctx.enter_context(tc.tile_pool(name="rope_pool", bufs=2))
        out_pool = ctx.enter_context(tc.tile_pool(name="out_pool", bufs=2))
        psum_x = ctx.enter_context(tc.psum_pool(name="psum_x", bufs=2))
        psum_c = ctx.enter_context(tc.psum_pool(name="psum_c", bufs=1))
        psum_kv = ctx.enter_context(tc.psum_pool(name="psum_kv", bufs=4))

        x_raw = [raw.tile([P, D_MODEL], BF16, name="x_raw%d" % i) for i in range(TOKEN_TILES)]
        wa_raw = raw.tile([P, X_PASSES, PACK, LATENT + ROPE], BF16)
        wb_raw = raw.tile([P, WB_PIECES, PACK, HEADS // WB_PIECES * (NOPE + VDIM)], BF16)
        nc.sync.dma_start(out=x_raw[0][:], in_=x_rows[span(0, P), :])
        for g in range(X_PASSES):
            nc.sync.dma_start(
                out=wa_raw[:, g, :, :], in_=Wkva[span(g, K_PASS), :].rearrange("(p j) c -> p j c", j=PACK)
            )
        wb_by_partition = Wkvb.rearrange("(t p) n -> p t n", p=P)
        for piece in range(WB_PIECES):
            nc.sync.dma_start(
                out=wb_raw[:, piece, :, :],
                in_=wb_by_partition[:, :, span(piece, HEADS // WB_PIECES * (NOPE + VDIM))],
            )
        for i in range(1, TOKEN_TILES):
            nc.sync.dma_start(out=x_raw[i][:], in_=x_rows[span(i, P), :])

        ident = const.tile([P, P], F32)
        make_identity(nc, ident[:])

        freq = const.tile([P, PAIRS], F32)
        nc.vector.memset(freq[:, 0:1], 1.0)
        for doubling in range(6):
            w = 2**doubling
            nc.vector.tensor_scalar(
                out=freq[:, w : 2 * w],
                in0=freq[:, 0:w],
                scalar1=ROPE_BASE ** (-2.0 * w / ROPE),
                scalar2=None,
                op0=ALU.mult,
            )
        position = const.tile([P, 2], F32)
        nc.gpsimd.iota(
            position[:], pattern=[[P, 2]], base=0, channel_multiplier=1, allow_small_or_imprecise_dtypes=True
        )
        turns = const.tile([P, 2 * 2 * PAIRS], F32)
        turns_view = turns[:].rearrange("p (f h j) -> p f h j", f=2, h=2)
        for half in range(2):
            nc.vector.tensor_scalar(
                out=turns_view[:, 0, half, :],
                in0=freq[:],
                scalar1=position[:, half : half + 1],
                scalar2=1.0 / (2.0 * math.pi),
                op0=ALU.mult,
                op1=ALU.mult,
            )
        nc.vector.tensor_scalar(
            out=turns[:, 2 * PAIRS :], in0=turns[:, : 2 * PAIRS], scalar1=0.25, scalar2=None, op0=ALU.add
        )
        whole_turns = const.tile([P, 2 * 2 * PAIRS], F32)
        nc.vector.tensor_scalar(
            out=whole_turns[:],
            in0=turns[:],
            scalar1=ROUND_MAGIC,
            scalar2=ROUND_MAGIC,
            op0=ALU.add,
            op1=ALU.subtract,
        )
        part_turns = const.tile([P, 2 * 2 * PAIRS], F32)
        nc.vector.tensor_tensor(out=part_turns[:], in0=turns[:], in1=whole_turns[:], op=ALU.subtract)
        trig = const.tile([P, 2 * 2 * PAIRS], F32)
        nc.scalar.activation(
            out=trig[:], in_=part_turns[:], func=mybir.ActivationFunctionType.Sin, scale=2.0 * math.pi
        )
        trig_view = trig[:].rearrange("p (f h j) -> p f h j", f=2, h=2)

        wa_codes = const.tile([P, X_PASSES * LATENT], U32, align_bytes=64)
        wa_scales = const.tile([P, X_PASSES * LATENT], U8, align_bytes=64)
        wr_codes = const.tile([P, X_PASSES * ROPE], U32, align_bytes=64)
        wr_scales = const.tile([P, X_PASSES * ROPE], U8, align_bytes=64)
        wb_codes = const.tile([P, 2 * HEADS * NOPE], U32, align_bytes=64)
        wb_scales = const.tile([P, 2 * HEADS * NOPE], U8, align_bytes=64)

        def quantise_unit(columns, codes, scales):
            grouped = stage.tile([P, UNIT], BF16, align_bytes=64)
            target = grouped[:].rearrange("p (n c i j) -> p n c j i", n=4, i=RUN, j=PACK)
            source = columns.rearrange("p n (c i) j -> p n c j i", i=RUN)
            nc.vector.tensor_copy(out=target[:, 0:2], in_=source[:, 0:2])
            for n in range(2, 4):
                nc.scalar.copy(out=target[:, n], in_=source[:, n])
            nc.vector.quantize_mx(out=codes.bitcast(FP8X4), scales=scales, in_=grouped[:])

        def quantise_wkva():
            for g in range(X_PASSES):
                quantise_unit(
                    wa_raw[:, g, :, :LATENT].rearrange("p j (n c) -> p n c j", c=P),
                    wa_codes[:, span(g, LATENT)],
                    wa_scales[:, span(g, LATENT)],
                )
            quantise_unit(wa_raw[:, :, :, LATENT:].rearrange("p g j c -> p g c j"), wr_codes[:], wr_scales[:])

        def quantise_wkvb():
            groups = HEAD_GROUPS // WB_PIECES
            for kind in range(2):
                for q in range(HEAD_GROUPS):
                    heads = wb_raw[:, q // groups, :, :].rearrange("p t (h k c) -> p k h c t", k=2, c=NOPE)
                    quantise_unit(
                        heads[:, kind, span(q % groups, HEAD_GROUP)],
                        wb_codes[:, span(kind * HEAD_GROUPS + q, BANK)],
                        wb_scales[:, span(kind * HEAD_GROUPS + q, BANK)],
                    )

        x_quantised = {}
        c_quantised = {}
        kf_tiles = {}

        def prepare(i):
            words = x_raw[i][:].bitcast(F32).rearrange("r (g p u) -> r g u p", g=X_PASSES, u=2)
            x_grouped = x_pool.tile([P, D_MODEL], BF16, align_bytes=64)
            grouped_words = x_grouped[:].bitcast(F32).rearrange("p (g r u) -> p g r u", g=X_PASSES, u=2)
            for bank in range(2):
                x_t = psum_x.tile([P, 2, 2, P], F32)
                for g in range(2):
                    for u in range(2):
                        nc.tensor.transpose(out=x_t[:, g, u, :], in_=words[:, 2 * bank + g, u, :], identity=ident[:])
                nc.vector.tensor_copy(
                    out=grouped_words[:, span(bank, 2), :, :], in_=x_t[:].rearrange("p g u r -> p g r u")
                )
            x_codes = x_pool.tile([P, X_PASSES * P], U32, align_bytes=64)
            x_scales = x_pool.tile([P, X_PASSES * P], U8, align_bytes=64)
            nc.vector.quantize_mx(out=x_codes[:].bitcast(FP8X4), scales=x_scales[:], in_=x_grouped[:])
            x_quantised[i] = (x_codes, x_scales)

        def project(i):
            x_codes, x_scales = x_quantised[i]
            c_t = psum_c.tile([P, PACK, P], F32)
            for t in range(PACK):
                for g in range(X_PASSES):
                    nc.tensor.matmul_mx(
                        out=c_t[:, t, :],
                        lhsT=wa_codes[:, span(g * PACK + t, P)].bitcast(FP8X4),
                        lhsT_scale=wa_scales[:, span(g * PACK + t, P)],
                        rhs=x_codes[:, span(g, P)].bitcast(FP8X4),
                        rhs_scale=x_scales[:, span(g, P)],
                        start=(g == 0),
                        stop=(g == X_PASSES - 1),
                    )
            k_pe = psum_c.tile([P, ROPE], F32)
            for g in range(X_PASSES):
                nc.tensor.matmul_mx(
                    out=k_pe[:],
                    lhsT=x_codes[:, span(g, P)].bitcast(FP8X4),
                    lhsT_scale=x_scales[:, span(g, P)],
                    rhs=wr_codes[:, span(g, ROPE)].bitcast(FP8X4),
                    rhs_scale=wr_scales[:, span(g, ROPE)],
                    start=(g == 0),
                    stop=(g == X_PASSES - 1),
                )
            c_grouped = c_pool.tile([P, P, PACK], BF16, align_bytes=64)
            nc.vector.tensor_copy(out=c_grouped[:], in_=c_t[:].rearrange("p t r -> p r t"))
            c_codes = c_pool.tile([P, P], U32, align_bytes=64)
            c_scales = c_pool.tile([P, P], U8, align_bytes=64)
            nc.vector.quantize_mx(
                out=c_codes[:].bitcast(FP8X4), scales=c_scales[:], in_=c_grouped[:].rearrange("p r t -> p (r t)")
            )
            c_quantised[i] = (c_codes, c_scales)

            half = i % 2
            sin = trig_view[:, 0, half, :].unsqueeze(2).to_broadcast([P, PAIRS, 2])
            cos = trig_view[:, 1, half, :].unsqueeze(2).to_broadcast([P, PAIRS, 2])
            pairs = k_pe[:].rearrange("p (j e) -> p j e", e=2)
            by_cos = rope_pool.tile([P, PAIRS, 2], F32)
            by_sin = rope_pool.tile([P, PAIRS, 2], F32)
            rotated = rope_pool.tile([P, PAIRS, 2], F32)
            nc.vector.tensor_tensor(out=by_cos[:], in0=pairs, in1=cos, op=ALU.mult)
            nc.vector.tensor_tensor(out=by_sin[:], in0=pairs, in1=sin, op=ALU.mult)
            nc.vector.tensor_tensor(out=rotated[:, :, 0], in0=by_cos[:, :, 0], in1=by_sin[:, :, 1], op=ALU.subtract)
            nc.vector.tensor_tensor(out=rotated[:, :, 1], in0=by_sin[:, :, 0], in1=by_cos[:, :, 1], op=ALU.add)
            kf_tile = out_pool.tile([P, HEADS, NOPE + ROPE], F32, bufs=3)
            nc.vector.tensor_copy(
                out=kf_tile[:, :, NOPE:],
                in_=rotated[:].rearrange("p j e -> p (j e)").unsqueeze(1).to_broadcast([P, HEADS, ROPE]),
            )
            kf_tiles[i] = kf_tile

        def expand(i):
            c_codes, c_scales = c_quantised[i]
            kf_tile = kf_tiles[i]
            v_tile = out_pool.tile([P, HEADS, VDIM], F32)
            for kind in range(2):
                for q in range(HEAD_GROUPS):
                    kv = psum_kv.tile([P, HEAD_GROUP, NOPE], F32)
                    nc.tensor.matmul_mx(
                        out=kv[:].rearrange("p h c -> p (h c)"),
                        lhsT=c_codes[:].bitcast(FP8X4),
                        lhsT_scale=c_scales[:],
                        rhs=wb_codes[:, span(kind * HEAD_GROUPS + q, BANK)].bitcast(FP8X4),
                        rhs_scale=wb_scales[:, span(kind * HEAD_GROUPS + q, BANK)],
                        start=True,
                        stop=True,
                    )
                    if kind == 0:
                        nc.scalar.copy(out=kf_tile[:, span(q, HEAD_GROUP), :NOPE], in_=kv[:])
                    else:
                        nc.scalar.copy(out=v_tile[:, span(q, HEAD_GROUP), :], in_=kv[:])
                if kind == 0:
                    nc.sync.dma_start(out=kf_rows[span(i, P), :], in_=kf_tile[:].rearrange("p h d -> p (h d)"))
                else:
                    nc.sync.dma_start(out=v_rows[span(i, P), :], in_=v_tile[:].rearrange("p h d -> p (h d)"))

        prepare(0)
        quantise_wkva()
        project(0)
        prepare(1)
        quantise_wkvb()
        for i in range(TOKEN_TILES):
            if i + 2 < TOKEN_TILES:
                prepare(i + 2)
            if i + 1 < TOKEN_TILES:
                project(i + 1)
            expand(i)
